import numpy as np
import ml_dtypes


def mxq(x, axis, fmt="e4m3"):
    dtype, down = {"e4m3": (ml_dtypes.float8_e4m3fn, 7), "e5m2": (ml_dtypes.float8_e5m2, 14)}[fmt]
    v = np.moveaxis(np.asarray(x, np.float32).astype(ml_dtypes.bfloat16).astype(np.float64), axis, -1)
    blocks = v.reshape(v.shape[:-1] + (-1, 32))
    amax = np.abs(blocks).max(-1, keepdims=True)
    byte = np.maximum(np.where(amax > 0, np.frexp(amax)[1] - 1 + 127, 0) - down, 1)
    scale = np.exp2(byte - 127.0)
    codes = (blocks / scale).astype(np.float32).astype(dtype).astype(np.float64)
    return np.moveaxis((codes * scale).reshape(v.shape), -1, axis)


WIDE = False


def mx_kscale(k):
    if not WIDE:
        return np.ones(k)
    levels = np.array([10, -10, 5, -5, 0])
    a = np.random.permutation(np.resize(levels, k // 512 * 4)).reshape(k // 512, 4)
    idx = np.arange(k)
    return np.exp2(a[idx // 512, idx % 128 // 32])


BF16 = ml_dtypes.bfloat16


def bf(x):
    return np.asarray(x, np.float32).astype(BF16)


def f64(x):
    return np.asarray(x).astype(np.float64)


B, N, DIM, HEADS, MID = 4, 128, 1024, 8, 512


def conprefix(xq, dw, db, uw, ub):
    h = np.tanh((xq @ mxq(f64(dw), 1, "e4m3").T) + f64(db))
    kv = (mxq(h, 2, "e4m3") @ mxq(f64(uw), 1, "e4m3").T) + f64(ub)
    return np.concatenate([np.zeros((B, N, DIM)), kv], axis=-1)


def setup_inputs():
    s = mx_kscale(DIM)
    a, m = 1.0 / np.sqrt(DIM), 1.0 / np.sqrt(MID)
    return {
        "x": bf(np.random.standard_normal((B, N, DIM)) * s),
        "Wqkv": bf(np.random.standard_normal((3 * DIM, DIM)) * a / s),
        "down_w": bf(np.random.standard_normal((MID, DIM)) * a / s),
        "down_b": bf(np.random.standard_normal(MID) * 0.3),
        "up_w": bf(np.random.standard_normal((2 * DIM, MID)) * m),
        "up_b": bf(np.random.standard_normal(2 * DIM) * 0.3),
        "pdown_w": bf(np.random.standard_normal((MID, DIM)) * a / s),
        "pdown_b": bf(np.random.standard_normal(MID) * 0.3),
        "pup_w": bf(np.random.standard_normal((2 * DIM, MID)) * m),
        "pup_b": bf(np.random.standard_normal(2 * DIM) * 0.3),
    }


def reference(x, Wqkv, down_w, down_b, up_w, up_b, pdown_w, pdown_b, pup_w, pup_b):
    xq = mxq(f64(x), 2, "e4m3")
    qkv = xq @ mxq(f64(Wqkv), 1, "e4m3").T
    return (qkv + conprefix(xq, pdown_w, pdown_b, pup_w, pup_b)
                + conprefix(xq, down_w, down_b, up_w, up_b))

@@ -1,0 +1,269 @@
+from contextlib import ExitStack
+
+import concourse.mybir as mybir
+from concourse.masks import make_identity
+
+F32 = mybir.dt.float32
+BF16 = mybir.dt.bfloat16
+U32 = mybir.dt.uint32
+U8 = mybir.dt.uint8
+FP8X4 = mybir.dt.float8_e4m3fn_x4
+
+P = 128
+TOKENS = 512
+DIM = 1024
+MID = 512
+QUERY = 1024
+KV = 2048
+PACK = 4
+K_PASS = P * PACK
+HALVES = 2
+CHUNK = 512
+ROW_TILES = CHUNK // P
+PASSES = 2
+BLOCK = PASSES * K_PASS * ROW_TILES
+ADAPTERS = 2
+
+FLOPS = 2 * TOKENS * ((QUERY + KV) * DIM + ADAPTERS * MID * DIM + ADAPTERS * KV * MID)
+
+
+def four_rows_a_partition(rows):
+    return rows.rearrange("(p j) k -> p (j k)", j=ROW_TILES)
+
+
+def tile_attention_pa_kernel(
+    tc, x, Wqkv, down_w, down_b, up_w, up_b, pdown_w, pdown_b, pup_w, pup_b, out
+):
+    nc = tc.nc
+    down_weights = (pdown_w, down_w)
+    down_biases = (pdown_b, down_b)
+    up_weights = (pup_w, up_w)
+    up_biases = (pup_b, up_b)
+    out_tiles = out.flatten_outer_dims().rearrange("(r j) f -> j r f", j=ROW_TILES)
+
+    with ExitStack() as ctx:
+        ctx.enter_context(tc.manual_schedule())
+        const = ctx.enter_context(tc.tile_pool(name="const", bufs=1))
+        raw = ctx.enter_context(tc.tile_pool(name="raw", bufs=1))
+        stage = ctx.enter_context(tc.tile_pool(name="stage", bufs=2))
+        keep = ctx.enter_context(tc.tile_pool(name="keep", bufs=1))
+        rotate = ctx.enter_context(tc.tile_pool(name="rotate", bufs=3))
+        hidden = ctx.enter_context(tc.tile_pool(name="hidden", bufs=ADAPTERS))
+        results = ctx.enter_context(
+            tc.tile_pool(name="results", bufs=ROW_TILES * (QUERY + KV) // CHUNK)
+        )
+        psum_t = ctx.enter_context(tc.psum_pool(name="psum_t", bufs=4))
+        psum_m = ctx.enter_context(tc.psum_pool(name="psum_m", bufs=4))
+
+        identity = const.tile([P, P], F32, name="identity")
+        make_identity(nc, identity[:])
+        down_bias_rows = const.tile([P, 2 * P], BF16, name="down_bias_rows")
+        nc.vector.memset(down_bias_rows[:], 0.0)
+        up_bias_rows = const.tile([P, KV], BF16, name="up_bias_rows")
+        nc.vector.memset(up_bias_rows[:], 0.0)
+        ones = const.tile([P, P], BF16, name="ones")
+        nc.vector.memset(ones[:], 1.0)
+
+        for a in range(ADAPTERS):
+            nc.scalar.dma_start(
+                out=down_bias_rows[HALVES * a : HALVES * (a + 1), :],
+                in_=down_biases[a].rearrange("(u c) -> u c", u=HALVES),
+            )
+            nc.scalar.dma_start(
+                out=up_bias_rows[a : a + 1, :], in_=up_biases[a].rearrange("(o f) -> o f", o=1)
+            )
+
+        x_raw = raw.tile([P, BLOCK], BF16, name="x_raw")
+        nc.sync.dma_start(out=x_raw[:], in_=four_rows_a_partition(x.flatten_outer_dims()))
+        down_raw = []
+        for a in range(ADAPTERS):
+            tile_a = raw.tile([P, BLOCK], BF16, name="down_raw%d" % a)
+            nc.sync.dma_start(
+                out=tile_a[:].rearrange("p (u c) -> p u c", u=HALVES),
+                in_=down_weights[a].rearrange("(u p e) k -> p u (e k)", u=HALVES, e=2),
+            )
+            down_raw.append(tile_a)
+        base_raw = []
+        up_raw = []
+        for c in range((QUERY + KV) // CHUNK):
+            tile_c = raw.tile([P, BLOCK], BF16, name="base_raw%d" % c)
+            nc.sync.dma_start(
+                out=tile_c[:], in_=four_rows_a_partition(Wqkv[c * CHUNK : (c + 1) * CHUNK, :])
+            )
+            base_raw.append(tile_c)
+            if c * CHUNK >= QUERY:
+                kv_rows = slice(c * CHUNK - QUERY, (c + 1) * CHUNK - QUERY)
+                tile_u = raw.tile([P, BLOCK], BF16, name="up_raw%d" % c)
+                for a in range(ADAPTERS):
+                    nc.sync.dma_start(
+                        out=tile_u[:, a * BLOCK // ADAPTERS : (a + 1) * BLOCK // ADAPTERS],
+                        in_=four_rows_a_partition(up_weights[a][kv_rows, :]),
+                    )
+                up_raw.append(tile_u)
+
+        warm = const.tile([P, 1], F32, name="warm")
+        nc.scalar.activation(
+            out=warm[:], in_=ones[:, 0:1], func=mybir.ActivationFunctionType.Tanh
+        )
+
+        def transpose_block(words):
+            grouped = stage.tile([P, BLOCK], BF16, name="grouped", align_bytes=64)
+            pairs = grouped[:].bitcast(F32).rearrange("p (g n u) -> p g n u", g=PASSES, u=HALVES)
+            for j in range(ROW_TILES):
+                bank = psum_t.tile([P, PASSES, HALVES, P], F32, name="bank")
+                for g in range(PASSES):
+                    for u in range(HALVES):
+                        nc.tensor.transpose(
+                            bank[:, g, u, :], words[:, j, g, u * P : (u + 1) * P], identity[:]
+                        )
+                nc.scalar.copy(
+                    out=pairs[:, :, j * P : (j + 1) * P, :],
+                    in_=bank[:].rearrange("p g u r -> p g r u"),
+                )
+            return grouped
+
+        def quantise_block(grouped, pool, label):
+            codes = pool.tile([P, PASSES * CHUNK], U32, name=label + "_codes", align_bytes=64)
+            scales = pool.tile([P, PASSES * CHUNK], U8, name=label + "_scales", align_bytes=64)
+            nc.vector.quantize_mx(out=codes[:].bitcast(FP8X4), scales=scales[:], in_=grouped[:])
+            return codes, scales
+
+        def mx_pass(acc, stationary, m, moving, g, start, stop):
+            s_cols = slice(g * CHUNK + m * P, g * CHUNK + (m + 1) * P)
+            m_cols = slice(g * CHUNK, (g + 1) * CHUNK)
+            nc.tensor.matmul_mx(
+                out=acc[:],
+                lhsT=stationary[0][:, s_cols].bitcast(FP8X4),
+                lhsT_scale=stationary[1][:, s_cols],
+                rhs=moving[0][:, m_cols].bitcast(FP8X4),
+                rhs_scale=moving[1][:, m_cols],
+                start=start,
+                stop=stop,
+            )
+
+        down_bias = const.tile([P, ADAPTERS * ROW_TILES], F32, name="down_bias")
+        kv_bias = const.tile([P, KV], F32, name="kv_bias")
+
+        def prepare_biases():
+            bias_bank = psum_m.tile([P, CHUNK], F32, name="acc")
+            nc.tensor.transpose(bias_bank[:, 0:P], down_bias_rows[:].bitcast(F32), identity[:])
+            down_bias_words = const.tile([P, ADAPTERS * HALVES], F32, name="down_bias_words")
+            nc.vector.tensor_copy(out=down_bias_words[:], in_=bias_bank[:, 0 : ADAPTERS * HALVES])
+            nc.vector.tensor_copy(out=down_bias[:], in_=down_bias_words[:].bitcast(BF16))
+            for c in range(KV // CHUNK):
+                cols = slice(c * CHUNK, (c + 1) * CHUNK)
+                bias_bank = psum_m.tile([P, CHUNK], F32, name="acc")
+                nc.tensor.matmul(
+                    out=bias_bank[:], lhsT=ones[:], rhs=up_bias_rows[:, cols], start=True, stop=True
+                )
+                nc.vector.tensor_copy(out=kv_bias[:, cols], in_=bias_bank[:])
+
+        operand = {}
+        h_rows = {}
+        kv_acc = {}
+        h_grouped = keep.tile([P, BLOCK], BF16, name="h_grouped", align_bytes=64)
+
+        def down_products(a):
+            h_rows[a] = hidden.tile([P, ROW_TILES, TOKENS], BF16, name="h_rows")
+            for t in range(ROW_TILES):
+                acc = psum_m.tile([P, CHUNK], F32, name="acc")
+                for g in range(PASSES):
+                    mx_pass(acc, operand["down", a], t, operand["x", 0], g, g == 0, g == PASSES - 1)
+                nc.scalar.activation(
+                    out=h_rows[a][:, t, :],
+                    in_=acc[:],
+                    func=mybir.ActivationFunctionType.Tanh,
+                    bias=down_bias[:, a * ROW_TILES + t : a * ROW_TILES + t + 1],
+                    scale=1.0,
+                )
+
+        def group_hidden(a):
+            nc.vector.tensor_copy(
+                out=h_grouped[:, a * BLOCK // ADAPTERS : (a + 1) * BLOCK // ADAPTERS].rearrange(
+                    "p (n t) -> p n t", t=PACK
+                ),
+                in_=h_rows[a][:].rearrange("p t n -> p n t"),
+            )
+
+        def store(result, j, c):
+            nc.sync.dma_start(out=out_tiles[j, :, c * CHUNK : (c + 1) * CHUNK], in_=result[:])
+
+        def in_output_order(columns):
+            return columns.rearrange("p (j r) -> p r j", j=ROW_TILES)
+
+        def as_written(columns):
+            return columns.rearrange("p (r j) -> p r j", j=ROW_TILES)
+
+        def query_products(c):
+            for j in range(ROW_TILES):
+                acc = psum_m.tile([P, CHUNK], F32, name="acc")
+                for g in range(PASSES):
+                    mx_pass(acc, operand["x", 0], j, operand["base", c], g, g == 0, g == PASSES - 1)
+                result = results.tile([P, CHUNK], F32, name="result")
+                nc.vector.tensor_copy(out=as_written(result[:]), in_=in_output_order(acc[:]))
+                store(result, j, c)
+
+        def kv_base_products(c):
+            for j in range(ROW_TILES):
+                kv_acc[j] = psum_m.tile([P, CHUNK], F32, name="acc")
+                for g in range(PASSES):
+                    mx_pass(kv_acc[j], operand["x", 0], j, operand["base", c], g, g == 0, False)
+
+        def kv_adapter_products(c):
+            bias_cols = slice(c * CHUNK - QUERY, (c + 1) * CHUNK - QUERY)
+            for j in range(ROW_TILES):
+                for a in range(ADAPTERS):
+                    mx_pass(kv_acc[j], operand["h", 0], j, operand["up", c], a, False, a == ADAPTERS - 1)
+                result = results.tile([P, CHUNK], F32, name="result")
+                nc.vector.tensor_tensor(
+                    out=as_written(result[:]),
+                    in0=in_output_order(kv_acc[j][:]),
+                    in1=as_written(kv_bias[:, bias_cols]),
+                    op=mybir.AluOpType.add,
+                )
+                store(result, j, c)
+
+        def rows_of_two_passes(tile_):
+            return tile_[:].bitcast(F32).rearrange("p (j g w) -> p j g w", j=ROW_TILES, g=PASSES)
+
+        def rows_of_one_pass_twice(tile_):
+            return tile_[:].bitcast(F32).rearrange("p (g j w) -> p j g w", j=ROW_TILES, g=PASSES)
+
+        blocks = [(("x", 0), rows_of_two_passes(x_raw))]
+        for a in range(ADAPTERS):
+            blocks.append((("down", a), rows_of_two_passes(down_raw[a])))
+        for c in range((QUERY + KV) // CHUNK):
+            blocks.append((("base", c), rows_of_two_passes(base_raw[c])))
+            if c * CHUNK >= QUERY:
+                blocks.append((("up", c), rows_of_one_pass_twice(up_raw[c - QUERY // CHUNK])))
+
+        def multiply(name):
+            kind, index = name
+            if kind == "x":
+                prepare_biases()
+            elif kind == "down":
+                down_products(index)
+            elif kind == "up":
+                kv_adapter_products(index)
+            elif kind == "base" and index * CHUNK < QUERY:
+                query_products(index)
+            elif kind == "base":
+                kv_base_products(index)
+
+        grouped = {}
+        for step in range(len(blocks) + 3):
+            if step < len(blocks):
+                grouped[step] = transpose_block(blocks[step][1])
+            if 0 <= step - 1 < len(blocks):
+                name = blocks[step - 1][0]
+                if name[0] == "x":
+                    operand[name] = quantise_block(grouped[step - 1], keep, "x")
+                else:
+                    operand[name] = quantise_block(grouped[step - 1], rotate, "w")
+            if 0 <= step - 2 < len(blocks):
+                multiply(blocks[step - 2][0])
+            if 0 <= step - 3 < len(blocks) and blocks[step - 3][0][0] == "down":
+                a = blocks[step - 3][0][1]
+                group_hidden(a)
+                if a == ADAPTERS - 1:
+                    operand["h", 0] = quantise_block(h_grouped, keep, "h")

@@ -57,21 +57,25 @@ def tile_attention_pa_kernel(
 
         identity = const.tile([P, P], F32, name="identity")
         make_identity(nc, identity[:])
-        down_bias_rows = const.tile([P, 2 * P], BF16, name="down_bias_rows")
-        nc.vector.memset(down_bias_rows[:], 0.0)
-        up_bias_rows = const.tile([P, KV], BF16, name="up_bias_rows")
-        nc.vector.memset(up_bias_rows[:], 0.0)
         ones = const.tile([P, P], BF16, name="ones")
         nc.vector.memset(ones[:], 1.0)
 
+        up_bias_in = const.tile([ADAPTERS, KV], BF16, name="up_bias_in")
+        down_bias_in = const.tile([ADAPTERS * HALVES, 2 * P], BF16, name="down_bias_in")
         for a in range(ADAPTERS):
             nc.scalar.dma_start(
-                out=down_bias_rows[HALVES * a : HALVES * (a + 1), :],
-                in_=down_biases[a].rearrange("(u c) -> u c", u=HALVES),
+                out=up_bias_in[a : a + 1, :], in_=up_biases[a].rearrange("(o f) -> o f", o=1)
             )
             nc.scalar.dma_start(
-                out=up_bias_rows[a : a + 1, :], in_=up_biases[a].rearrange("(o f) -> o f", o=1)
+                out=down_bias_in[HALVES * a : HALVES * (a + 1), :],
+                in_=down_biases[a].rearrange("(u c) -> u c", u=HALVES),
             )
+        up_bias_rows = const.tile([P, KV], BF16, name="up_bias_rows")
+        nc.vector.memset(up_bias_rows[:], 0.0)
+        nc.vector.tensor_copy(out=up_bias_rows[0:ADAPTERS, :], in_=up_bias_in[:])
+        down_bias_rows = const.tile([P, 2 * P], BF16, name="down_bias_rows")
+        nc.vector.memset(down_bias_rows[:], 0.0)
+        nc.vector.tensor_copy(out=down_bias_rows[0 : ADAPTERS * HALVES, :], in_=down_bias_in[:])
 
         x_raw = raw.tile([P, BLOCK], BF16, name="x_raw")
         nc.sync.dma_start(out=x_raw[:], in_=four_rows_a_partition(x.flatten_outer_dims()))
@@ -144,19 +148,20 @@ def tile_attention_pa_kernel(
         down_bias = const.tile([P, ADAPTERS * ROW_TILES], F32, name="down_bias")
         kv_bias = const.tile([P, KV], F32, name="kv_bias")
 
-        def prepare_biases():
+        def prepare_down_biases():
             bias_bank = psum_m.tile([P, CHUNK], F32, name="acc")
             nc.tensor.transpose(bias_bank[:, 0:P], down_bias_rows[:].bitcast(F32), identity[:])
             down_bias_words = const.tile([P, ADAPTERS * HALVES], F32, name="down_bias_words")
             nc.vector.tensor_copy(out=down_bias_words[:], in_=bias_bank[:, 0 : ADAPTERS * HALVES])
             nc.vector.tensor_copy(out=down_bias[:], in_=down_bias_words[:].bitcast(BF16))
-            for c in range(KV // CHUNK):
-                cols = slice(c * CHUNK, (c + 1) * CHUNK)
-                bias_bank = psum_m.tile([P, CHUNK], F32, name="acc")
-                nc.tensor.matmul(
-                    out=bias_bank[:], lhsT=ones[:], rhs=up_bias_rows[:, cols], start=True, stop=True
-                )
-                nc.vector.tensor_copy(out=kv_bias[:, cols], in_=bias_bank[:])
+
+        def spread_kv_bias(c):
+            cols = slice(c * CHUNK, (c + 1) * CHUNK)
+            bias_bank = psum_m.tile([P, CHUNK], F32, name="acc")
+            nc.tensor.matmul(
+                out=bias_bank[:], lhsT=ones[:], rhs=up_bias_rows[:, cols], start=True, stop=True
+            )
+            nc.vector.tensor_copy(out=kv_bias[:, cols], in_=bias_bank[:])
 
         operand = {}
         h_rows = {}
@@ -240,7 +245,7 @@ def tile_attention_pa_kernel(
         def multiply(name):
             kind, index = name
             if kind == "x":
-                prepare_biases()
+                prepare_down_biases()
             elif kind == "down":
                 down_products(index)
             elif kind == "up":
@@ -260,6 +265,8 @@ def tile_attention_pa_kernel(
                     operand[name] = quantise_block(grouped[step - 1], keep, "x")
                 else:
                     operand[name] = quantise_block(grouped[step - 1], rotate, "w")
+            if step < KV // CHUNK:
+                spread_kv_bias(step)
             if 0 <= step - 2 < len(blocks):
                 multiply(blocks[step - 2][0])
             if 0 <= step - 3 < len(blocks) and blocks[step - 3][0][0] == "down":

@@ -23,6 +23,7 @@ ROW_TILES = CHUNK // P
 PASSES = 2
 BLOCK = PASSES * K_PASS * ROW_TILES
 ADAPTERS = 2
+RUNS_PER_STEP = 2
 
 FLOPS = 2 * TOKENS * ((QUERY + KV) * DIM + ADAPTERS * MID * DIM + ADAPTERS * KV * MID)
 
@@ -110,10 +111,9 @@ def tile_attention_pa_kernel(
             out=warm[:], in_=ones[:, 0:1], func=mybir.ActivationFunctionType.Tanh
         )
 
-        def transpose_block(words):
-            grouped = stage.tile([P, BLOCK], BF16, name="grouped", align_bytes=64)
+        def transpose_rows(words, grouped, tiles):
             pairs = grouped[:].bitcast(F32).rearrange("p (g n u) -> p g n u", g=PASSES, u=HALVES)
-            for j in range(ROW_TILES):
+            for j in tiles:
                 bank = psum_t.tile([P, PASSES, HALVES, P], F32, name="bank")
                 for g in range(PASSES):
                     for u in range(HALVES):
@@ -124,7 +124,6 @@ def tile_attention_pa_kernel(
                     out=pairs[:, :, j * P : (j + 1) * P, :],
                     in_=bank[:].rearrange("p g u r -> p g r u"),
                 )
-            return grouped
 
         def quantise_block(grouped, pool, label):
             codes = pool.tile([P, PASSES * CHUNK], U32, name=label + "_codes", align_bytes=64)
@@ -168,9 +167,10 @@ def tile_attention_pa_kernel(
         kv_acc = {}
         h_grouped = keep.tile([P, BLOCK], BF16, name="h_grouped", align_bytes=64)
 
-        def down_products(a):
-            h_rows[a] = hidden.tile([P, ROW_TILES, TOKENS], BF16, name="h_rows")
-            for t in range(ROW_TILES):
+        def down_products(a, tiles):
+            if 0 in tiles:
+                h_rows[a] = hidden.tile([P, ROW_TILES, TOKENS], BF16, name="h_rows")
+            for t in tiles:
                 acc = psum_m.tile([P, CHUNK], F32, name="acc")
                 for g in range(PASSES):
                     mx_pass(acc, operand["down", a], t, operand["x", 0], g, g == 0, g == PASSES - 1)
@@ -199,8 +199,8 @@ def tile_attention_pa_kernel(
         def as_written(columns):
             return columns.rearrange("p (r j) -> p r j", j=ROW_TILES)
 
-        def query_products(c):
-            for j in range(ROW_TILES):
+        def query_products(c, tiles):
+            for j in tiles:
                 acc = psum_m.tile([P, CHUNK], F32, name="acc")
                 for g in range(PASSES):
                     mx_pass(acc, operand["x", 0], j, operand["base", c], g, g == 0, g == PASSES - 1)
@@ -208,15 +208,15 @@ def tile_attention_pa_kernel(
                 nc.vector.tensor_copy(out=as_written(result[:]), in_=in_output_order(acc[:]))
                 store(result, j, c)
 
-        def kv_base_products(c):
-            for j in range(ROW_TILES):
+        def kv_base_products(c, tiles):
+            for j in tiles:
                 kv_acc[j] = psum_m.tile([P, CHUNK], F32, name="acc")
                 for g in range(PASSES):
                     mx_pass(kv_acc[j], operand["x", 0], j, operand["base", c], g, g == 0, False)
 
-        def kv_adapter_products(c):
+        def kv_adapter_products(c, tiles):
             bias_cols = slice(c * CHUNK - QUERY, (c + 1) * CHUNK - QUERY)
-            for j in range(ROW_TILES):
+            for j in tiles:
                 for a in range(ADAPTERS):
                     mx_pass(kv_acc[j], operand["h", 0], j, operand["up", c], a, False, a == ADAPTERS - 1)
                 result = results.tile([P, CHUNK], F32, name="result")
@@ -242,33 +242,39 @@ def tile_attention_pa_kernel(
             if c * CHUNK >= QUERY:
                 blocks.append((("up", c), rows_of_one_pass_twice(up_raw[c - QUERY // CHUNK])))
 
-        def multiply(name):
+        def multiply(name, tiles):
             kind, index = name
-            if kind == "x":
+            if kind == "x" and 0 in tiles:
                 prepare_down_biases()
             elif kind == "down":
-                down_products(index)
+                down_products(index, tiles)
             elif kind == "up":
-                kv_adapter_products(index)
+                kv_adapter_products(index, tiles)
             elif kind == "base" and index * CHUNK < QUERY:
-                query_products(index)
+                query_products(index, tiles)
             elif kind == "base":
-                kv_base_products(index)
+                kv_base_products(index, tiles)
 
         grouped = {}
         for step in range(len(blocks) + 3):
             if step < len(blocks):
-                grouped[step] = transpose_block(blocks[step][1])
+                grouped[step] = stage.tile([P, BLOCK], BF16, name="grouped", align_bytes=64)
             if 0 <= step - 1 < len(blocks):
                 name = blocks[step - 1][0]
                 if name[0] == "x":
                     operand[name] = quantise_block(grouped[step - 1], keep, "x")
                 else:
                     operand[name] = quantise_block(grouped[step - 1], rotate, "w")
-            if step < KV // CHUNK:
-                spread_kv_bias(step)
-            if 0 <= step - 2 < len(blocks):
-                multiply(blocks[step - 2][0])
+            for run in range(RUNS_PER_STEP):
+                tiles = range(
+                    run * ROW_TILES // RUNS_PER_STEP, (run + 1) * ROW_TILES // RUNS_PER_STEP
+                )
+                if step < len(blocks):
+                    transpose_rows(blocks[step][1], grouped[step], tiles)
+                if step < KV // CHUNK and run == RUNS_PER_STEP - 1:
+                    spread_kv_bias(step)
+                if 0 <= step - 2 < len(blocks):
+                    multiply(blocks[step - 2][0], tiles)
             if 0 <= step - 3 < len(blocks) and blocks[step - 3][0][0] == "down":
                 a = blocks[step - 3][0][1]
                 group_hidden(a)

@@ -23,7 +23,7 @@ ROW_TILES = CHUNK // P
 PASSES = 2
 BLOCK = PASSES * K_PASS * ROW_TILES
 ADAPTERS = 2
-RUNS_PER_STEP = 2
+BANKS = 8
 
 FLOPS = 2 * TOKENS * ((QUERY + KV) * DIM + ADAPTERS * MID * DIM + ADAPTERS * KV * MID)
 
@@ -46,47 +46,57 @@ def tile_attention_pa_kernel(
         ctx.enter_context(tc.manual_schedule())
         const = ctx.enter_context(tc.tile_pool(name="const", bufs=1))
         raw = ctx.enter_context(tc.tile_pool(name="raw", bufs=1))
-        stage = ctx.enter_context(tc.tile_pool(name="stage", bufs=2))
+        stage = ctx.enter_context(tc.tile_pool(name="stage", bufs=3))
         keep = ctx.enter_context(tc.tile_pool(name="keep", bufs=1))
-        rotate = ctx.enter_context(tc.tile_pool(name="rotate", bufs=3))
+        rotate = ctx.enter_context(tc.tile_pool(name="rotate", bufs=5))
         hidden = ctx.enter_context(tc.tile_pool(name="hidden", bufs=ADAPTERS))
-        results = ctx.enter_context(
-            tc.tile_pool(name="results", bufs=ROW_TILES * (QUERY + KV) // CHUNK)
-        )
-        psum_t = ctx.enter_context(tc.psum_pool(name="psum_t", bufs=4))
-        psum_m = ctx.enter_context(tc.psum_pool(name="psum_m", bufs=4))
+        results = ctx.enter_context(tc.tile_pool(name="results", bufs=16))
+        psum = ctx.enter_context(tc.psum_pool(name="psum", bufs=BANKS))
 
         identity = const.tile([P, P], F32, name="identity")
         make_identity(nc, identity[:])
+
         ones = const.tile([P, P], BF16, name="ones")
         nc.vector.memset(ones[:], 1.0)
+        warm = const.tile([P, 1], F32, name="warm")
+        nc.scalar.activation(
+            out=warm[:], in_=ones[:, 0:1], func=mybir.ActivationFunctionType.Tanh
+        )
 
-        up_bias_in = const.tile([ADAPTERS, KV], BF16, name="up_bias_in")
-        down_bias_in = const.tile([ADAPTERS * HALVES, 2 * P], BF16, name="down_bias_in")
+        down_bias_rows = const.tile([P, 2 * P], BF16, name="down_bias_rows")
+        nc.vector.memset(down_bias_rows[:].bitcast(U32), 0)
+        up_bias_rows = const.tile([P, KV], BF16, name="up_bias_rows")
+        nc.vector.memset(up_bias_rows[:].bitcast(U32), 0)
         for a in range(ADAPTERS):
-            nc.scalar.dma_start(
-                out=up_bias_in[a : a + 1, :], in_=up_biases[a].rearrange("(o f) -> o f", o=1)
-            )
-            nc.scalar.dma_start(
-                out=down_bias_in[HALVES * a : HALVES * (a + 1), :],
+            nc.gpsimd.dma_start(
+                out=down_bias_rows[HALVES * a : HALVES * (a + 1), :],
                 in_=down_biases[a].rearrange("(u c) -> u c", u=HALVES),
             )
-        up_bias_rows = const.tile([P, KV], BF16, name="up_bias_rows")
-        nc.vector.memset(up_bias_rows[:], 0.0)
-        nc.vector.tensor_copy(out=up_bias_rows[0:ADAPTERS, :], in_=up_bias_in[:])
-        down_bias_rows = const.tile([P, 2 * P], BF16, name="down_bias_rows")
-        nc.vector.memset(down_bias_rows[:], 0.0)
-        nc.vector.tensor_copy(out=down_bias_rows[0 : ADAPTERS * HALVES, :], in_=down_bias_in[:])
+        for a in range(ADAPTERS):
+            nc.gpsimd.dma_start(
+                out=up_bias_rows[a : a + 1, :], in_=up_biases[a].rearrange("(o f) -> o f", o=1)
+            )
 
         x_raw = raw.tile([P, BLOCK], BF16, name="x_raw")
-        nc.sync.dma_start(out=x_raw[:], in_=four_rows_a_partition(x.flatten_outer_dims()))
+        x_rows = four_rows_a_partition(x.flatten_outer_dims())
+        for half in range(2):
+            cols = slice(half * BLOCK // 2, (half + 1) * BLOCK // 2)
+            nc.sync.dma_start(out=x_raw[:, cols], in_=x_rows[:, cols])
         down_raw = []
         for a in range(ADAPTERS):
             tile_a = raw.tile([P, BLOCK], BF16, name="down_raw%d" % a)
-            nc.sync.dma_start(
-                out=tile_a[:].rearrange("p (u c) -> p u c", u=HALVES),
-                in_=down_weights[a].rearrange("(u p e) k -> p u (e k)", u=HALVES, e=2),
-            )
+            if a == 0:
+                for u in range(HALVES):
+                    rows = down_weights[a][u * 2 * P : (u + 1) * 2 * P, :]
+                    nc.sync.dma_start(
+                        out=tile_a[:, u * BLOCK // 2 : (u + 1) * BLOCK // 2],
+                        in_=rows.rearrange("(p e) k -> p (e k)", e=2),
+                    )
+            else:
+                nc.sync.dma_start(
+                    out=tile_a[:].rearrange("p (u c) -> p u c", u=HALVES),
+                    in_=down_weights[a].rearrange("(u p e) k -> p u (e k)", u=HALVES, e=2),
+                )
             down_raw.append(tile_a)
         base_raw = []
         up_raw = []
@@ -106,30 +116,68 @@ def tile_attention_pa_kernel(
                     )
                 up_raw.append(tile_u)
 
-        warm = const.tile([P, 1], F32, name="warm")
-        nc.scalar.activation(
-            out=warm[:], in_=ones[:, 0:1], func=mybir.ActivationFunctionType.Tanh
-        )
+        def rows_of_two_passes(tile_):
+            return tile_[:].bitcast(F32).rearrange("p (j g w) -> p j g w", j=ROW_TILES, g=PASSES)
 
-        def transpose_rows(words, grouped, tiles):
-            pairs = grouped[:].bitcast(F32).rearrange("p (g n u) -> p g n u", g=PASSES, u=HALVES)
-            for j in tiles:
-                bank = psum_t.tile([P, PASSES, HALVES, P], F32, name="bank")
-                for g in range(PASSES):
-                    for u in range(HALVES):
-                        nc.tensor.transpose(
-                            bank[:, g, u, :], words[:, j, g, u * P : (u + 1) * P], identity[:]
-                        )
-                nc.scalar.copy(
-                    out=pairs[:, :, j * P : (j + 1) * P, :],
-                    in_=bank[:].rearrange("p g u r -> p g r u"),
-                )
+        def rows_of_one_pass_twice(tile_):
+            return tile_[:].bitcast(F32).rearrange("p (g j w) -> p j g w", j=ROW_TILES, g=PASSES)
 
-        def quantise_block(grouped, pool, label):
+        words = {("x", 0): rows_of_two_passes(x_raw)}
+        for a in range(ADAPTERS):
+            words["down", a] = rows_of_two_passes(down_raw[a])
+        for c in range((QUERY + KV) // CHUNK):
+            words["base", c] = rows_of_two_passes(base_raw[c])
+            if c * CHUNK >= QUERY:
+                words["up", c] = rows_of_one_pass_twice(up_raw[c - QUERY // CHUNK])
+
+        grouped = {}
+        operand = {}
+
+        def transpose_tile(name, j, on_vector):
+            pairs = grouped[name][:].bitcast(F32).rearrange(
+                "p (g n u) -> p g n u", g=PASSES, u=HALVES
+            )
+            bank = psum.tile([P, PASSES, HALVES, P], F32, name="bank")
+            for g in range(PASSES):
+                for u in range(HALVES):
+                    nc.tensor.transpose(
+                        bank[:, g, u, :], words[name][:, j, g, u * P : (u + 1) * P], identity[:]
+                    )
+            target = pairs[:, :, j * P : (j + 1) * P, :]
+            source = bank[:].rearrange("p g u r -> p g r u")
+            if on_vector:
+                nc.vector.tensor_copy(out=target, in_=source)
+            else:
+                nc.scalar.copy(out=target, in_=source)
+
+        def transpose_block(name, vector_tiles=()):
+            grouped[name] = stage.tile([P, BLOCK], BF16, name="grouped", align_bytes=64)
+            for j in range(ROW_TILES):
+                transpose_tile(name, j, j in vector_tiles)
+
+        def quantise(name, source, pool, label):
             codes = pool.tile([P, PASSES * CHUNK], U32, name=label + "_codes", align_bytes=64)
             scales = pool.tile([P, PASSES * CHUNK], U8, name=label + "_scales", align_bytes=64)
-            nc.vector.quantize_mx(out=codes[:].bitcast(FP8X4), scales=scales[:], in_=grouped[:])
-            return codes, scales
+            nc.vector.quantize_mx(out=codes[:].bitcast(FP8X4), scales=scales[:], in_=source[:])
+            operand[name] = (codes, scales)
+
+        def quantise_weights(name):
+            quantise(name, grouped[name], rotate, "w")
+
+        def transpose_and_quantise_by_tile(name, pool, label):
+            grouped[name] = stage.tile([P, BLOCK], BF16, name="grouped", align_bytes=64)
+            codes = pool.tile([P, PASSES * CHUNK], U32, name=label + "_codes", align_bytes=64)
+            scales = pool.tile([P, PASSES * CHUNK], U8, name=label + "_scales", align_bytes=64)
+            operand[name] = (codes, scales)
+            for j in range(ROW_TILES):
+                transpose_tile(name, j, False)
+                for g in range(PASSES):
+                    cols = slice(g * CHUNK + j * P, g * CHUNK + (j + 1) * P)
+                    nc.vector.quantize_mx(
+                        out=codes[:, cols].bitcast(FP8X4),
+                        scales=scales[:, cols],
+                        in_=grouped[name][:, cols.start * PACK : cols.stop * PACK],
+                    )
 
         def mx_pass(acc, stationary, m, moving, g, start, stop):
             s_cols = slice(g * CHUNK + m * P, g * CHUNK + (m + 1) * P)
@@ -148,7 +196,7 @@ def tile_attention_pa_kernel(
         kv_bias = const.tile([P, KV], F32, name="kv_bias")
 
         def prepare_down_biases():
-            bias_bank = psum_m.tile([P, CHUNK], F32, name="acc")
+            bias_bank = psum.tile([P, CHUNK], F32, name="bank")
             nc.tensor.transpose(bias_bank[:, 0:P], down_bias_rows[:].bitcast(F32), identity[:])
             down_bias_words = const.tile([P, ADAPTERS * HALVES], F32, name="down_bias_words")
             nc.vector.tensor_copy(out=down_bias_words[:], in_=bias_bank[:, 0 : ADAPTERS * HALVES])
@@ -156,22 +204,19 @@ def tile_attention_pa_kernel(
 
         def spread_kv_bias(c):
             cols = slice(c * CHUNK, (c + 1) * CHUNK)
-            bias_bank = psum_m.tile([P, CHUNK], F32, name="acc")
+            bias_bank = psum.tile([P, CHUNK], F32, name="bank")
             nc.tensor.matmul(
                 out=bias_bank[:], lhsT=ones[:], rhs=up_bias_rows[:, cols], start=True, stop=True
             )
-            nc.vector.tensor_copy(out=kv_bias[:, cols], in_=bias_bank[:])
+            nc.scalar.copy(out=kv_bias[:, cols], in_=bias_bank[:])
 
-        operand = {}
         h_rows = {}
-        kv_acc = {}
         h_grouped = keep.tile([P, BLOCK], BF16, name="h_grouped", align_bytes=64)
 
-        def down_products(a, tiles):
-            if 0 in tiles:
-                h_rows[a] = hidden.tile([P, ROW_TILES, TOKENS], BF16, name="h_rows")
-            for t in tiles:
-                acc = psum_m.tile([P, CHUNK], F32, name="acc")
+        def down_products(a):
+            h_rows[a] = hidden.tile([P, ROW_TILES, TOKENS], BF16, name="h_rows")
+            for t in range(ROW_TILES):
+                acc = psum.tile([P, CHUNK], F32, name="bank")
                 for g in range(PASSES):
                     mx_pass(acc, operand["down", a], t, operand["x", 0], g, g == 0, g == PASSES - 1)
                 nc.scalar.activation(
@@ -199,84 +244,70 @@ def tile_attention_pa_kernel(
         def as_written(columns):
             return columns.rearrange("p (r j) -> p r j", j=ROW_TILES)
 
-        def query_products(c, tiles):
-            for j in tiles:
-                acc = psum_m.tile([P, CHUNK], F32, name="acc")
-                for g in range(PASSES):
-                    mx_pass(acc, operand["x", 0], j, operand["base", c], g, g == 0, g == PASSES - 1)
-                result = results.tile([P, CHUNK], F32, name="result")
-                nc.vector.tensor_copy(out=as_written(result[:]), in_=in_output_order(acc[:]))
-                store(result, j, c)
+        acc = {}
 
-        def kv_base_products(c, tiles):
-            for j in tiles:
-                kv_acc[j] = psum_m.tile([P, CHUNK], F32, name="acc")
-                for g in range(PASSES):
-                    mx_pass(kv_acc[j], operand["x", 0], j, operand["base", c], g, g == 0, False)
+        def multiply(c, j):
+            passes = [("x", "base", g) for g in range(PASSES)]
+            if c * CHUNK >= QUERY:
+                passes += [("h", "up", a) for a in range(ADAPTERS)]
+            acc[c, j] = psum.tile([P, CHUNK], F32, name="bank")
+            for i, (tokens, weights, g) in enumerate(passes):
+                mx_pass(
+                    acc[c, j], operand[tokens, 0], j, operand[weights, c], g,
+                    i == 0, i == len(passes) - 1,
+                )
 
-        def kv_adapter_products(c, tiles):
-            bias_cols = slice(c * CHUNK - QUERY, (c + 1) * CHUNK - QUERY)
-            for j in tiles:
-                for a in range(ADAPTERS):
-                    mx_pass(kv_acc[j], operand["h", 0], j, operand["up", c], a, False, a == ADAPTERS - 1)
-                result = results.tile([P, CHUNK], F32, name="result")
+        def finish(c, j, scalar=False):
+            result = results.tile([P, CHUNK], F32, name="result")
+            sums = in_output_order(acc[c, j][:])
+            if c * CHUNK >= QUERY:
                 nc.vector.tensor_tensor(
                     out=as_written(result[:]),
-                    in0=in_output_order(kv_acc[j][:]),
-                    in1=as_written(kv_bias[:, bias_cols]),
+                    in0=sums,
+                    in1=as_written(kv_bias[:, c * CHUNK - QUERY : (c + 1) * CHUNK - QUERY]),
                     op=mybir.AluOpType.add,
                 )
-                store(result, j, c)
+            elif scalar:
+                nc.scalar.copy(out=as_written(result[:]), in_=sums)
+            else:
+                nc.vector.tensor_copy(out=as_written(result[:]), in_=sums)
+            store(result, j, c)
 
-        def rows_of_two_passes(tile_):
-            return tile_[:].bitcast(F32).rearrange("p (j g w) -> p j g w", j=ROW_TILES, g=PASSES)
+        transpose_and_quantise_by_tile(("x", 0), keep, "x")
+        transpose_and_quantise_by_tile(("down", 0), rotate, "w")
+        prepare_down_biases()
+        down_products(0)
+        transpose_block(("down", 1), vector_tiles=(1, 3))
+        quantise_weights(("down", 1))
+        transpose_block(("base", 0))
+        group_hidden(0)
+        down_products(1)
+        quantise_weights(("base", 0))
+        transpose_block(("base", 1))
+        group_hidden(1)
+        quantise(("h", 0), h_grouped, keep, "h")
 
-        def rows_of_one_pass_twice(tile_):
-            return tile_[:].bitcast(F32).rearrange("p (g j w) -> p j g w", j=ROW_TILES, g=PASSES)
+        for j in range(ROW_TILES):
+            multiply(0, j)
+        for j in range(ROW_TILES):
+            finish(0, j, scalar=j % 2 == 1)
+        quantise_weights(("base", 1))
 
-        blocks = [(("x", 0), rows_of_two_passes(x_raw))]
-        for a in range(ADAPTERS):
-            blocks.append((("down", a), rows_of_two_passes(down_raw[a])))
-        for c in range((QUERY + KV) // CHUNK):
-            blocks.append((("base", c), rows_of_two_passes(base_raw[c])))
-            if c * CHUNK >= QUERY:
-                blocks.append((("up", c), rows_of_one_pass_twice(up_raw[c - QUERY // CHUNK])))
-
-        def multiply(name, tiles):
-            kind, index = name
-            if kind == "x" and 0 in tiles:
-                prepare_down_biases()
-            elif kind == "down":
-                down_products(index, tiles)
-            elif kind == "up":
-                kv_adapter_products(index, tiles)
-            elif kind == "base" and index * CHUNK < QUERY:
-                query_products(index, tiles)
-            elif kind == "base":
-                kv_base_products(index, tiles)
-
-        grouped = {}
-        for step in range(len(blocks) + 3):
-            if step < len(blocks):
-                grouped[step] = stage.tile([P, BLOCK], BF16, name="grouped", align_bytes=64)
-            if 0 <= step - 1 < len(blocks):
-                name = blocks[step - 1][0]
-                if name[0] == "x":
-                    operand[name] = quantise_block(grouped[step - 1], keep, "x")
-                else:
-                    operand[name] = quantise_block(grouped[step - 1], rotate, "w")
-            for run in range(RUNS_PER_STEP):
-                tiles = range(
-                    run * ROW_TILES // RUNS_PER_STEP, (run + 1) * ROW_TILES // RUNS_PER_STEP
-                )
-                if step < len(blocks):
-                    transpose_rows(blocks[step][1], grouped[step], tiles)
-                if step < KV // CHUNK and run == RUNS_PER_STEP - 1:
-                    spread_kv_bias(step)
-                if 0 <= step - 2 < len(blocks):
-                    multiply(blocks[step - 2][0], tiles)
-            if 0 <= step - 3 < len(blocks) and blocks[step - 3][0][0] == "down":
-                a = blocks[step - 3][0][1]
-                group_hidden(a)
-                if a == ADAPTERS - 1:
-                    operand["h", 0] = quantise_block(h_grouped, keep, "h")
+        last = (QUERY + KV) // CHUNK - 1
+        for c in range(QUERY // CHUNK, last + 1):
+            transpose_block(("base", c))
+            transpose_block(("up", c))
+            if c * CHUNK == QUERY:
+                for kv_chunk in range(KV // CHUNK):
+                    spread_kv_bias(kv_chunk)
+            for j in range(ROW_TILES):
+                multiply(c - 1, j)
+            quantise_weights(("base", c))
+            finish(c - 1, 0)
+            finish(c - 1, 1)
+            quantise_weights(("up", c))
+            finish(c - 1, 2)
+            finish(c - 1, 3)
+        for j in range(ROW_TILES):
+            multiply(last, j)
+            finish(last, j)

@@ -56,24 +56,23 @@ def tile_attention_pa_kernel(
         identity = const.tile([P, P], F32, name="identity")
         make_identity(nc, identity[:])
 
+        down_bias_rows = const.tile([P, 2 * P], BF16, name="down_bias_rows")
+        nc.vector.memset(down_bias_rows[:].bitcast(U32), 0)
+        for a in range(ADAPTERS):
+            nc.scalar.dma_start(
+                out=down_bias_rows[HALVES * a : HALVES * (a + 1), :],
+                in_=down_biases[a].rearrange("(u c) -> u c", u=HALVES),
+            )
         ones = const.tile([P, P], BF16, name="ones")
         nc.vector.memset(ones[:], 1.0)
         warm = const.tile([P, 1], F32, name="warm")
         nc.scalar.activation(
             out=warm[:], in_=ones[:, 0:1], func=mybir.ActivationFunctionType.Tanh
         )
-
-        down_bias_rows = const.tile([P, 2 * P], BF16, name="down_bias_rows")
-        nc.vector.memset(down_bias_rows[:].bitcast(U32), 0)
         up_bias_rows = const.tile([P, KV], BF16, name="up_bias_rows")
         nc.vector.memset(up_bias_rows[:].bitcast(U32), 0)
         for a in range(ADAPTERS):
-            nc.gpsimd.dma_start(
-                out=down_bias_rows[HALVES * a : HALVES * (a + 1), :],
-                in_=down_biases[a].rearrange("(u c) -> u c", u=HALVES),
-            )
-        for a in range(ADAPTERS):
-            nc.gpsimd.dma_start(
+            nc.scalar.dma_start(
                 out=up_bias_rows[a : a + 1, :], in_=up_biases[a].rearrange("(o f) -> o f", o=1)
             )
 
@@ -133,51 +132,47 @@ def tile_attention_pa_kernel(
         grouped = {}
         operand = {}
 
-        def transpose_tile(name, j, on_vector):
-            pairs = grouped[name][:].bitcast(F32).rearrange(
-                "p (g n u) -> p g n u", g=PASSES, u=HALVES
-            )
-            bank = psum.tile([P, PASSES, HALVES, P], F32, name="bank")
-            for g in range(PASSES):
+        def open_block(name, pool, label):
+            grouped[name] = stage.tile([P, BLOCK], BF16, name="grouped", align_bytes=64)
+            codes = pool.tile([P, PASSES * CHUNK], U32, name=label + "_codes", align_bytes=64)
+            scales = pool.tile([P, PASSES * CHUNK], U8, name=label + "_scales", align_bytes=64)
+            operand[name] = (codes, scales)
+
+        def transpose_pair(name, g, pair, on_vector=False):
+            bank = psum.tile([P, 2, HALVES, P], F32, name="bank")
+            for i in range(2):
                 for u in range(HALVES):
                     nc.tensor.transpose(
-                        bank[:, g, u, :], words[name][:, j, g, u * P : (u + 1) * P], identity[:]
+                        bank[:, i, u, :],
+                        words[name][:, 2 * pair + i, g, u * P : (u + 1) * P],
+                        identity[:],
                     )
-            target = pairs[:, :, j * P : (j + 1) * P, :]
-            source = bank[:].rearrange("p g u r -> p g r u")
+            first = g * CHUNK + 2 * pair * P
+            target = grouped[name][:].bitcast(F32)[:, first * HALVES : (first + 2 * P) * HALVES]
+            target = target.rearrange("p (i r u) -> p i r u", i=2, u=HALVES)
+            source = bank[:].rearrange("p i u r -> p i r u")
             if on_vector:
                 nc.vector.tensor_copy(out=target, in_=source)
             else:
                 nc.scalar.copy(out=target, in_=source)
 
-        def transpose_block(name, vector_tiles=()):
-            grouped[name] = stage.tile([P, BLOCK], BF16, name="grouped", align_bytes=64)
-            for j in range(ROW_TILES):
-                transpose_tile(name, j, j in vector_tiles)
+        def quantise_rows(name, first, rows):
+            codes, scales = operand[name]
+            cols = slice(first, first + rows)
+            nc.vector.quantize_mx(
+                out=codes[:, cols].bitcast(FP8X4),
+                scales=scales[:, cols],
+                in_=grouped[name][:, first * PACK : (first + rows) * PACK],
+            )
 
-        def quantise(name, source, pool, label):
-            codes = pool.tile([P, PASSES * CHUNK], U32, name=label + "_codes", align_bytes=64)
-            scales = pool.tile([P, PASSES * CHUNK], U8, name=label + "_scales", align_bytes=64)
-            nc.vector.quantize_mx(out=codes[:].bitcast(FP8X4), scales=scales[:], in_=source[:])
-            operand[name] = (codes, scales)
+        def quantise(name):
+            quantise_rows(name, 0, PASSES * CHUNK)
 
-        def quantise_weights(name):
-            quantise(name, grouped[name], rotate, "w")
-
-        def transpose_and_quantise_by_tile(name, pool, label):
-            grouped[name] = stage.tile([P, BLOCK], BF16, name="grouped", align_bytes=64)
-            codes = pool.tile([P, PASSES * CHUNK], U32, name=label + "_codes", align_bytes=64)
-            scales = pool.tile([P, PASSES * CHUNK], U8, name=label + "_scales", align_bytes=64)
-            operand[name] = (codes, scales)
-            for j in range(ROW_TILES):
-                transpose_tile(name, j, False)
-                for g in range(PASSES):
-                    cols = slice(g * CHUNK + j * P, g * CHUNK + (j + 1) * P)
-                    nc.vector.quantize_mx(
-                        out=codes[:, cols].bitcast(FP8X4),
-                        scales=scales[:, cols],
-                        in_=grouped[name][:, cols.start * PACK : cols.stop * PACK],
-                    )
+        def transpose_block(name, vector_pairs=()):
+            open_block(name, rotate, "w")
+            for g in range(PASSES):
+                for pair in range(2):
+                    transpose_pair(name, g, pair, (g, pair) in vector_pairs)
 
         def mx_pass(acc, stationary, m, moving, g, start, stop):
             s_cols = slice(g * CHUNK + m * P, g * CHUNK + (m + 1) * P)
@@ -212,6 +207,10 @@ def tile_attention_pa_kernel(
 
         h_rows = {}
         h_grouped = keep.tile([P, BLOCK], BF16, name="h_grouped", align_bytes=64)
+        h_operand = (
+            keep.tile([P, PASSES * CHUNK], U32, name="h_codes", align_bytes=64),
+            keep.tile([P, PASSES * CHUNK], U8, name="h_scales", align_bytes=64),
+        )
 
         def down_products(a):
             h_rows[a] = hidden.tile([P, ROW_TILES, TOKENS], BF16, name="h_rows")
@@ -273,25 +272,32 @@ def tile_attention_pa_kernel(
                 nc.vector.tensor_copy(out=as_written(result[:]), in_=sums)
             store(result, j, c)
 
-        transpose_and_quantise_by_tile(("x", 0), keep, "x")
-        transpose_and_quantise_by_tile(("down", 0), rotate, "w")
+        for name, pool, label in ((("x", 0), keep, "x"), (("down", 0), rotate, "w")):
+            open_block(name, pool, label)
+            for pair in range(2):
+                for g in range(PASSES):
+                    transpose_pair(name, g, pair, on_vector=False)
+                    quantise_rows(name, g * CHUNK + 2 * pair * P, 2 * P)
         prepare_down_biases()
         down_products(0)
-        transpose_block(("down", 1), vector_tiles=(1, 3))
-        quantise_weights(("down", 1))
+        transpose_block(("down", 1), vector_pairs=((0, 0), (0, 1), (1, 0)))
+        for g in range(PASSES):
+            quantise_rows(("down", 1), g * CHUNK, CHUNK)
         transpose_block(("base", 0))
         group_hidden(0)
         down_products(1)
-        quantise_weights(("base", 0))
+        quantise(("base", 0))
         transpose_block(("base", 1))
         group_hidden(1)
-        quantise(("h", 0), h_grouped, keep, "h")
+        grouped["h", 0] = h_grouped
+        operand["h", 0] = h_operand
+        quantise(("h", 0))
 
         for j in range(ROW_TILES):
             multiply(0, j)
         for j in range(ROW_TILES):
             finish(0, j, scalar=j % 2 == 1)
-        quantise_weights(("base", 1))
+        quantise(("base", 1))
 
         last = (QUERY + KV) // CHUNK - 1
         for c in range(QUERY // CHUNK, last + 1):
@@ -302,10 +308,10 @@ def tile_attention_pa_kernel(
                     spread_kv_bias(kv_chunk)
             for j in range(ROW_TILES):
                 multiply(c - 1, j)
-            quantise_weights(("base", c))
+            quantise(("base", c))
             finish(c - 1, 0)
             finish(c - 1, 1)
-            quantise_weights(("up", c))
+            quantise(("up", c))
             finish(c - 1, 2)
             finish(c - 1, 3)
         for j in range(ROW_TILES):

@@ -56,6 +56,23 @@ def tile_attention_pa_kernel(
         identity = const.tile([P, P], F32, name="identity")
         make_identity(nc, identity[:])
 
+        x_raw = raw.tile([P, BLOCK], BF16, name="x_raw")
+        x_rows = four_rows_a_partition(x.flatten_outer_dims())
+        for half in range(2):
+            cols = slice(half * BLOCK // 2, (half + 1) * BLOCK // 2)
+            nc.sync.dma_start(out=x_raw[:, cols], in_=x_rows[:, cols])
+        down_raw = []
+        for a in range(ADAPTERS):
+            tile_a = raw.tile([P, BLOCK], BF16, name="down_raw%d" % a)
+            if a == 0:
+                for u in range(HALVES):
+                    rows = down_weights[a][u * 2 * P : (u + 1) * 2 * P, :]
+                    nc.sync.dma_start(
+                        out=tile_a[:, u * BLOCK // 2 : (u + 1) * BLOCK // 2],
+                        in_=rows.rearrange("(p e) k -> p (e k)", e=2),
+                    )
+            down_raw.append(tile_a)
+
         down_bias_rows = const.tile([P, 2 * P], BF16, name="down_bias_rows")
         nc.vector.memset(down_bias_rows[:].bitcast(U32), 0)
         for a in range(ADAPTERS):
@@ -76,27 +93,10 @@ def tile_attention_pa_kernel(
                 out=up_bias_rows[a : a + 1, :], in_=up_biases[a].rearrange("(o f) -> o f", o=1)
             )
 
-        x_raw = raw.tile([P, BLOCK], BF16, name="x_raw")
-        x_rows = four_rows_a_partition(x.flatten_outer_dims())
-        for half in range(2):
-            cols = slice(half * BLOCK // 2, (half + 1) * BLOCK // 2)
-            nc.sync.dma_start(out=x_raw[:, cols], in_=x_rows[:, cols])
-        down_raw = []
-        for a in range(ADAPTERS):
-            tile_a = raw.tile([P, BLOCK], BF16, name="down_raw%d" % a)
-            if a == 0:
-                for u in range(HALVES):
-                    rows = down_weights[a][u * 2 * P : (u + 1) * 2 * P, :]
-                    nc.sync.dma_start(
-                        out=tile_a[:, u * BLOCK // 2 : (u + 1) * BLOCK // 2],
-                        in_=rows.rearrange("(p e) k -> p (e k)", e=2),
-                    )
-            else:
-                nc.sync.dma_start(
-                    out=tile_a[:].rearrange("p (u c) -> p u c", u=HALVES),
-                    in_=down_weights[a].rearrange("(u p e) k -> p u (e k)", u=HALVES, e=2),
-                )
-            down_raw.append(tile_a)
+        nc.sync.dma_start(
+            out=down_raw[1][:].rearrange("p (u c) -> p u c", u=HALVES),
+            in_=down_weights[1].rearrange("(u p e) k -> p u (e k)", u=HALVES, e=2),
+        )
         base_raw = []
         up_raw = []
         for c in range((QUERY + KV) // CHUNK):

@@ -24,6 +24,7 @@ PASSES = 2
 BLOCK = PASSES * K_PASS * ROW_TILES
 ADAPTERS = 2
 BANKS = 8
+BIAS_BEHIND = 3
 
 FLOPS = 2 * TOKENS * ((QUERY + KV) * DIM + ADAPTERS * MID * DIM + ADAPTERS * KV * MID)
 
@@ -86,34 +87,39 @@ def tile_attention_pa_kernel(
         nc.scalar.activation(
             out=warm[:], in_=ones[:, 0:1], func=mybir.ActivationFunctionType.Tanh
         )
-        up_bias_rows = const.tile([P, KV], BF16, name="up_bias_rows")
-        nc.vector.memset(up_bias_rows[:].bitcast(U32), 0)
-        for a in range(ADAPTERS):
-            nc.scalar.dma_start(
-                out=up_bias_rows[a : a + 1, :], in_=up_biases[a].rearrange("(o f) -> o f", o=1)
-            )
-
         nc.sync.dma_start(
             out=down_raw[1][:].rearrange("p (u c) -> p u c", u=HALVES),
             in_=down_weights[1].rearrange("(u p e) k -> p u (e k)", u=HALVES, e=2),
         )
+        last = (QUERY + KV) // CHUNK - 1
+
+        def load_chunk_rows(columns, rows, c):
+            if c == last:
+                columns = columns.rearrange("p (half k) -> p half k", half=HALVES)
+                rows = rows.rearrange("(half p e) k -> p half (e k)", half=HALVES, e=2)
+            else:
+                rows = four_rows_a_partition(rows)
+            nc.sync.dma_start(out=columns, in_=rows)
+
         base_raw = []
         up_raw = []
+        up_bias = const.tile([P, ADAPTERS * KV], BF16, name="up_bias")
         for c in range((QUERY + KV) // CHUNK):
             tile_c = raw.tile([P, BLOCK], BF16, name="base_raw%d" % c)
-            nc.sync.dma_start(
-                out=tile_c[:], in_=four_rows_a_partition(Wqkv[c * CHUNK : (c + 1) * CHUNK, :])
-            )
+            load_chunk_rows(tile_c[:], Wqkv[c * CHUNK : (c + 1) * CHUNK, :], c)
             base_raw.append(tile_c)
             if c * CHUNK >= QUERY:
                 kv_rows = slice(c * CHUNK - QUERY, (c + 1) * CHUNK - QUERY)
                 tile_u = raw.tile([P, BLOCK], BF16, name="up_raw%d" % c)
                 for a in range(ADAPTERS):
-                    nc.sync.dma_start(
-                        out=tile_u[:, a * BLOCK // ADAPTERS : (a + 1) * BLOCK // ADAPTERS],
-                        in_=four_rows_a_partition(up_weights[a][kv_rows, :]),
-                    )
+                    columns = tile_u[:, a * BLOCK // ADAPTERS : (a + 1) * BLOCK // ADAPTERS]
+                    load_chunk_rows(columns, up_weights[a][kv_rows, :], c)
                 up_raw.append(tile_u)
+            if c == BIAS_BEHIND:
+                for a in range(ADAPTERS):
+                    nc.sync.dma_start(
+                        out=up_bias[:, a * KV : (a + 1) * KV], in_=up_biases[a].partition_broadcast(P)
+                    )
 
         def rows_of_two_passes(tile_):
             return tile_[:].bitcast(F32).rearrange("p (j g w) -> p j g w", j=ROW_TILES, g=PASSES)
@@ -174,11 +180,11 @@ def tile_attention_pa_kernel(
                 for pair in range(2):
                     transpose_pair(name, g, pair, (g, pair) in vector_pairs)
 
-        def mx_pass(acc, stationary, m, moving, g, start, stop):
+        def mx_pass(acc, stationary, m, moving, g, start, stop, cols=range(CHUNK)):
             s_cols = slice(g * CHUNK + m * P, g * CHUNK + (m + 1) * P)
-            m_cols = slice(g * CHUNK, (g + 1) * CHUNK)
+            m_cols = slice(g * CHUNK + cols.start, g * CHUNK + cols.stop)
             nc.tensor.matmul_mx(
-                out=acc[:],
+                out=acc,
                 lhsT=stationary[0][:, s_cols].bitcast(FP8X4),
                 lhsT_scale=stationary[1][:, s_cols],
                 rhs=moving[0][:, m_cols].bitcast(FP8X4),
@@ -188,7 +194,6 @@ def tile_attention_pa_kernel(
             )
 
         down_bias = const.tile([P, ADAPTERS * ROW_TILES], F32, name="down_bias")
-        kv_bias = const.tile([P, KV], F32, name="kv_bias")
 
         def prepare_down_biases():
             bias_bank = psum.tile([P, CHUNK], F32, name="bank")
@@ -197,13 +202,17 @@ def tile_attention_pa_kernel(
             nc.vector.tensor_copy(out=down_bias_words[:], in_=bias_bank[:, 0 : ADAPTERS * HALVES])
             nc.vector.tensor_copy(out=down_bias[:], in_=down_bias_words[:].bitcast(BF16))
 
-        def spread_kv_bias(c):
-            cols = slice(c * CHUNK, (c + 1) * CHUNK)
-            bias_bank = psum.tile([P, CHUNK], F32, name="bank")
-            nc.tensor.matmul(
-                out=bias_bank[:], lhsT=ones[:], rhs=up_bias_rows[:, cols], start=True, stop=True
+        kv_bias = {}
+
+        def add_biases(c):
+            kv_bias[c] = const.tile([P, CHUNK], F32, name="kv_bias%d" % c)
+            first = c * CHUNK - QUERY
+            nc.vector.tensor_tensor(
+                out=kv_bias[c][:],
+                in0=up_bias[:, first : first + CHUNK],
+                in1=up_bias[:, KV + first : KV + first + CHUNK],
+                op=mybir.AluOpType.add,
             )
-            nc.scalar.copy(out=kv_bias[:, cols], in_=bias_bank[:])
 
         h_rows = {}
         h_grouped = keep.tile([P, BLOCK], BF16, name="h_grouped", align_bytes=64)
@@ -217,7 +226,7 @@ def tile_attention_pa_kernel(
             for t in range(ROW_TILES):
                 acc = psum.tile([P, CHUNK], F32, name="bank")
                 for g in range(PASSES):
-                    mx_pass(acc, operand["down", a], t, operand["x", 0], g, g == 0, g == PASSES - 1)
+                    mx_pass(acc[:], operand["down", a], t, operand["x", 0], g, g == 0, g == PASSES - 1)
                 nc.scalar.activation(
                     out=h_rows[a][:, t, :],
                     in_=acc[:],
@@ -234,43 +243,49 @@ def tile_attention_pa_kernel(
                 in_=h_rows[a][:].rearrange("p t n -> p n t"),
             )
 
-        def store(result, j, c):
-            nc.sync.dma_start(out=out_tiles[j, :, c * CHUNK : (c + 1) * CHUNK], in_=result[:])
+        def in_output_order(columns, tiles=ROW_TILES):
+            return columns.rearrange("p (j r) -> p r j", j=tiles)
 
-        def in_output_order(columns):
-            return columns.rearrange("p (j r) -> p r j", j=ROW_TILES)
-
-        def as_written(columns):
-            return columns.rearrange("p (r j) -> p r j", j=ROW_TILES)
+        def as_written(columns, tiles=ROW_TILES):
+            return columns.rearrange("p (r j) -> p r j", j=tiles)
 
         acc = {}
 
-        def multiply(c, j):
+        def multiply(c, j, cols=range(CHUNK)):
             passes = [("x", "base", g) for g in range(PASSES)]
             if c * CHUNK >= QUERY:
                 passes += [("h", "up", a) for a in range(ADAPTERS)]
             acc[c, j] = psum.tile([P, CHUNK], F32, name="bank")
             for i, (tokens, weights, g) in enumerate(passes):
                 mx_pass(
-                    acc[c, j], operand[tokens, 0], j, operand[weights, c], g,
-                    i == 0, i == len(passes) - 1,
+                    acc[c, j][:, 0 : len(cols)], operand[tokens, 0], j, operand[weights, c], g,
+                    i == 0, i == len(passes) - 1, cols,
                 )
 
-        def finish(c, j, scalar=False):
+        def finish(c, j, scalar=False, cols=range(CHUNK)):
+            tiles = 2 if c == last else ROW_TILES
             result = results.tile([P, CHUNK], F32, name="result")
-            sums = in_output_order(acc[c, j][:])
-            if c * CHUNK >= QUERY:
-                nc.vector.tensor_tensor(
-                    out=as_written(result[:]),
-                    in0=sums,
-                    in1=as_written(kv_bias[:, c * CHUNK - QUERY : (c + 1) * CHUNK - QUERY]),
-                    op=mybir.AluOpType.add,
-                )
-            elif scalar:
-                nc.scalar.copy(out=as_written(result[:]), in_=sums)
-            else:
-                nc.vector.tensor_copy(out=as_written(result[:]), in_=sums)
-            store(result, j, c)
+            first = c * CHUNK + cols.start
+            halves = range(cols.start, cols.stop, CHUNK // 2) if c == last else (cols.start,)
+            width = CHUNK // 2 if c == last else CHUNK
+            for start in halves:
+                at = slice(start - cols.start, start - cols.start + width)
+                target = as_written(result[:, at], tiles)
+                sums = in_output_order(acc[c, j][:, at], tiles)
+                if c * CHUNK >= QUERY:
+                    nc.vector.tensor_tensor(
+                        out=target,
+                        in0=sums,
+                        in1=as_written(kv_bias[c][:, start : start + width], tiles),
+                        op=mybir.AluOpType.add,
+                    )
+                elif scalar:
+                    nc.scalar.copy(out=target, in_=sums)
+                else:
+                    nc.vector.tensor_copy(out=target, in_=sums)
+            nc.sync.dma_start(
+                out=out_tiles[j, :, first : first + len(cols)], in_=result[:, 0 : len(cols)]
+            )
 
         for name, pool, label in ((("x", 0), keep, "x"), (("down", 0), rotate, "w")):
             open_block(name, pool, label)
@@ -288,32 +303,60 @@ def tile_attention_pa_kernel(
         down_products(1)
         quantise(("base", 0))
         transpose_block(("base", 1))
+        transpose_block(("base", 2))
         group_hidden(1)
         grouped["h", 0] = h_grouped
         operand["h", 0] = h_operand
-        quantise(("h", 0))
 
         for j in range(ROW_TILES):
             multiply(0, j)
-        for j in range(ROW_TILES):
-            finish(0, j, scalar=j % 2 == 1)
         quantise(("base", 1))
+        for j in range(ROW_TILES):
+            multiply(1, j)
+        finish(0, 0)
+        finish(0, 1, scalar=True)
+        finish(0, 2)
+        finish(0, 3, scalar=True)
+        quantise(("base", 2))
+        finish(1, 0)
+        finish(1, 1, scalar=True)
+        finish(1, 2)
+        finish(1, 3, scalar=True)
+        quantise(("h", 0))
 
-        last = (QUERY + KV) // CHUNK - 1
-        for c in range(QUERY // CHUNK, last + 1):
+        transpose_block(("up", 2))
+        transpose_block(("base", 3))
+        transpose_block(("up", 3))
+        quantise(("up", 2))
+        for j in range(ROW_TILES):
+            multiply(2, j)
+        quantise(("base", 3))
+        add_biases(2)
+        finish(2, 0)
+        quantise(("up", 3))
+        for j in range(ROW_TILES):
+            multiply(3, j)
+        for j in range(1, ROW_TILES):
+            finish(2, j)
+        add_biases(3)
+        for j in range(ROW_TILES):
+            finish(3, j)
+        add_biases(4)
+        add_biases(5)
+        for c in (4, 5):
             transpose_block(("base", c))
             transpose_block(("up", c))
-            if c * CHUNK == QUERY:
-                for kv_chunk in range(KV // CHUNK):
-                    spread_kv_bias(kv_chunk)
-            for j in range(ROW_TILES):
-                multiply(c - 1, j)
-            quantise(("base", c))
-            finish(c - 1, 0)
-            finish(c - 1, 1)
-            quantise(("up", c))
-            finish(c - 1, 2)
-            finish(c - 1, 3)
+        quantise(("base", 4))
+        quantise(("up", 4))
         for j in range(ROW_TILES):
-            multiply(last, j)
-            finish(last, j)
+            multiply(4, j)
+        quantise(("base", 5))
+        finish(4, 0)
+        quantise(("up", 5))
+        for j in range(1, ROW_TILES):
+            finish(4, j)
+        for j in range(ROW_TILES):
+            width = CHUNK if j < ROW_TILES - 1 else CHUNK // 2
+            for first in range(0, CHUNK, width):
+                multiply(last, j, range(first, first + width))
+                finish(last, j, cols=range(first, first + width))

@@ -303,58 +303,31 @@ def tile_attention_pa_kernel(
         down_products(1)
         quantise(("base", 0))
         transpose_block(("base", 1))
-        transpose_block(("base", 2))
         group_hidden(1)
         grouped["h", 0] = h_grouped
         operand["h", 0] = h_operand
+        quantise(("h", 0))
 
         for j in range(ROW_TILES):
             multiply(0, j)
+        for j in range(ROW_TILES):
+            finish(0, j, scalar=j % 2 == 1)
         quantise(("base", 1))
-        for j in range(ROW_TILES):
-            multiply(1, j)
-        finish(0, 0)
-        finish(0, 1, scalar=True)
-        finish(0, 2)
-        finish(0, 3, scalar=True)
-        quantise(("base", 2))
-        finish(1, 0)
-        finish(1, 1, scalar=True)
-        finish(1, 2)
-        finish(1, 3, scalar=True)
-        quantise(("h", 0))
 
-        transpose_block(("up", 2))
-        transpose_block(("base", 3))
-        transpose_block(("up", 3))
-        quantise(("up", 2))
-        for j in range(ROW_TILES):
-            multiply(2, j)
-        quantise(("base", 3))
-        add_biases(2)
-        finish(2, 0)
-        quantise(("up", 3))
-        for j in range(ROW_TILES):
-            multiply(3, j)
-        for j in range(1, ROW_TILES):
-            finish(2, j)
-        add_biases(3)
-        for j in range(ROW_TILES):
-            finish(3, j)
-        add_biases(4)
-        add_biases(5)
-        for c in (4, 5):
-            transpose_block(("base", c))
-            transpose_block(("up", c))
-        quantise(("base", 4))
-        quantise(("up", 4))
-        for j in range(ROW_TILES):
-            multiply(4, j)
-        quantise(("base", 5))
-        finish(4, 0)
-        quantise(("up", 5))
-        for j in range(1, ROW_TILES):
-            finish(4, j)
+        for c in range(QUERY // CHUNK, last + 1):
+            transpose_block(("base", c), ())
+            quantise(("base", c))
+            transpose_block(("up", c), ())
+            for j in range(ROW_TILES):
+                multiply(c - 1, j)
+            if c > QUERY // CHUNK:
+                add_biases(c - 1)
+            finish(c - 1, 0)
+            finish(c - 1, 1, scalar=True)
+            quantise(("up", c))
+            finish(c - 1, 2)
+            finish(c - 1, 3, scalar=True)
+        add_biases(last)
         for j in range(ROW_TILES):
             width = CHUNK if j < ROW_TILES - 1 else CHUNK // 2
             for first in range(0, CHUNK, width):

from contextlib import ExitStack

import concourse.mybir as mybir
from concourse.masks import make_identity

F32 = mybir.dt.float32
BF16 = mybir.dt.bfloat16
U32 = mybir.dt.uint32
U8 = mybir.dt.uint8
FP8X4 = mybir.dt.float8_e4m3fn_x4

P = 128
TOKENS = 512
DIM = 1024
MID = 512
QUERY = 1024
KV = 2048
PACK = 4
K_PASS = P * PACK
HALVES = 2
CHUNK = 512
ROW_TILES = CHUNK // P
PASSES = 2
BLOCK = PASSES * K_PASS * ROW_TILES
ADAPTERS = 2
BANKS = 8
BIAS_BEHIND = 3

FLOPS = 2 * TOKENS * ((QUERY + KV) * DIM + ADAPTERS * MID * DIM + ADAPTERS * KV * MID)


def four_rows_a_partition(rows):
    return rows.rearrange("(p j) k -> p (j k)", j=ROW_TILES)


def tile_attention_pa_kernel(
    tc, x, Wqkv, down_w, down_b, up_w, up_b, pdown_w, pdown_b, pup_w, pup_b, out
):
    nc = tc.nc
    down_weights = (pdown_w, down_w)
    down_biases = (pdown_b, down_b)
    up_weights = (pup_w, up_w)
    up_biases = (pup_b, up_b)
    out_tiles = out.flatten_outer_dims().rearrange("(r j) f -> j r f", j=ROW_TILES)

    with ExitStack() as ctx:
        ctx.enter_context(tc.manual_schedule())
        const = ctx.enter_context(tc.tile_pool(name="const", bufs=1))
        raw = ctx.enter_context(tc.tile_pool(name="raw", bufs=1))
        stage = ctx.enter_context(tc.tile_pool(name="stage", bufs=3))
        keep = ctx.enter_context(tc.tile_pool(name="keep", bufs=1))
        rotate = ctx.enter_context(tc.tile_pool(name="rotate", bufs=5))
        hidden = ctx.enter_context(tc.tile_pool(name="hidden", bufs=ADAPTERS))
        results = ctx.enter_context(tc.tile_pool(name="results", bufs=16))
        psum = ctx.enter_context(tc.psum_pool(name="psum", bufs=BANKS))

        identity = const.tile([P, P], F32, name="identity")
        make_identity(nc, identity[:])

        x_raw = raw.tile([P, BLOCK], BF16, name="x_raw")
        x_rows = four_rows_a_partition(x.flatten_outer_dims())
        for half in range(2):
            cols = slice(half * BLOCK // 2, (half + 1) * BLOCK // 2)
            nc.sync.dma_start(out=x_raw[:, cols], in_=x_rows[:, cols])
        down_raw = []
        for a in range(ADAPTERS):
            tile_a = raw.tile([P, BLOCK], BF16, name="down_raw%d" % a)
            if a == 0:
                for u in range(HALVES):
                    rows = down_weights[a][u * 2 * P : (u + 1) * 2 * P, :]
                    nc.sync.dma_start(
                        out=tile_a[:, u * BLOCK // 2 : (u + 1) * BLOCK // 2],
                        in_=rows.rearrange("(p e) k -> p (e k)", e=2),
                    )
            down_raw.append(tile_a)

        down_bias_rows = const.tile([P, 2 * P], BF16, name="down_bias_rows")
        nc.vector.memset(down_bias_rows[:].bitcast(U32), 0)
        for a in range(ADAPTERS):
            nc.scalar.dma_start(
                out=down_bias_rows[HALVES * a : HALVES * (a + 1), :],
                in_=down_biases[a].rearrange("(u c) -> u c", u=HALVES),
            )
        ones = const.tile([P, P], BF16, name="ones")
        nc.vector.memset(ones[:], 1.0)
        warm = const.tile([P, 1], F32, name="warm")
        nc.scalar.activation(
            out=warm[:], in_=ones[:, 0:1], func=mybir.ActivationFunctionType.Tanh
        )
        nc.sync.dma_start(
            out=down_raw[1][:].rearrange("p (u c) -> p u c", u=HALVES),
            in_=down_weights[1].rearrange("(u p e) k -> p u (e k)", u=HALVES, e=2),
        )
        last = (QUERY + KV) // CHUNK - 1

        def load_chunk_rows(columns, rows, c):
            if c == last:
                columns = columns.rearrange("p (half k) -> p half k", half=HALVES)
                rows = rows.rearrange("(half p e) k -> p half (e k)", half=HALVES, e=2)
            else:
                rows = four_rows_a_partition(rows)
            nc.sync.dma_start(out=columns, in_=rows)

        base_raw = []
        up_raw = []
        up_bias = const.tile([P, ADAPTERS * KV], BF16, name="up_bias")
        for c in range((QUERY + KV) // CHUNK):
            tile_c = raw.tile([P, BLOCK], BF16, name="base_raw%d" % c)
            load_chunk_rows(tile_c[:], Wqkv[c * CHUNK : (c + 1) * CHUNK, :], c)
            base_raw.append(tile_c)
            if c * CHUNK >= QUERY:
                kv_rows = slice(c * CHUNK - QUERY, (c + 1) * CHUNK - QUERY)
                tile_u = raw.tile([P, BLOCK], BF16, name="up_raw%d" % c)
                for a in range(ADAPTERS):
                    columns = tile_u[:, a * BLOCK // ADAPTERS : (a + 1) * BLOCK // ADAPTERS]
                    load_chunk_rows(columns, up_weights[a][kv_rows, :], c)
                up_raw.append(tile_u)
            if c == BIAS_BEHIND:
                for a in range(ADAPTERS):
                    nc.sync.dma_start(
                        out=up_bias[:, a * KV : (a + 1) * KV], in_=up_biases[a].partition_broadcast(P)
                    )

        def rows_of_two_passes(tile_):
            return tile_[:].bitcast(F32).rearrange("p (j g w) -> p j g w", j=ROW_TILES, g=PASSES)

        def rows_of_one_pass_twice(tile_):
            return tile_[:].bitcast(F32).rearrange("p (g j w) -> p j g w", j=ROW_TILES, g=PASSES)

        words = {("x", 0): rows_of_two_passes(x_raw)}
        for a in range(ADAPTERS):
            words["down", a] = rows_of_two_passes(down_raw[a])
        for c in range((QUERY + KV) // CHUNK):
            words["base", c] = rows_of_two_passes(base_raw[c])
            if c * CHUNK >= QUERY:
                words["up", c] = rows_of_one_pass_twice(up_raw[c - QUERY // CHUNK])

        grouped = {}
        operand = {}

        def open_block(name, pool, label):
            grouped[name] = stage.tile([P, BLOCK], BF16, name="grouped", align_bytes=64)
            codes = pool.tile([P, PASSES * CHUNK], U32, name=label + "_codes", align_bytes=64)
            scales = pool.tile([P, PASSES * CHUNK], U8, name=label + "_scales", align_bytes=64)
            operand[name] = (codes, scales)

        def transpose_pair(name, g, pair, on_vector=False):
            bank = psum.tile([P, 2, HALVES, P], F32, name="bank")
            for i in range(2):
                for u in range(HALVES):
                    nc.tensor.transpose(
                        bank[:, i, u, :],
                        words[name][:, 2 * pair + i, g, u * P : (u + 1) * P],
                        identity[:],
                    )
            first = g * CHUNK + 2 * pair * P
            target = grouped[name][:].bitcast(F32)[:, first * HALVES : (first + 2 * P) * HALVES]
            target = target.rearrange("p (i r u) -> p i r u", i=2, u=HALVES)
            source = bank[:].rearrange("p i u r -> p i r u")
            if on_vector:
                nc.vector.tensor_copy(out=target, in_=source)
            else:
                nc.scalar.copy(out=target, in_=source)

        def quantise_rows(name, first, rows):
            codes, scales = operand[name]
            cols = slice(first, first + rows)
            nc.vector.quantize_mx(
                out=codes[:, cols].bitcast(FP8X4),
                scales=scales[:, cols],
                in_=grouped[name][:, first * PACK : (first + rows) * PACK],
            )

        def quantise(name):
            quantise_rows(name, 0, PASSES * CHUNK)

        def transpose_block(name, vector_pairs=()):
            open_block(name, rotate, "w")
            for g in range(PASSES):
                for pair in range(2):
                    transpose_pair(name, g, pair, (g, pair) in vector_pairs)

        def mx_pass(acc, stationary, m, moving, g, start, stop, cols=range(CHUNK)):
            s_cols = slice(g * CHUNK + m * P, g * CHUNK + (m + 1) * P)
            m_cols = slice(g * CHUNK + cols.start, g * CHUNK + cols.stop)
            nc.tensor.matmul_mx(
                out=acc,
                lhsT=stationary[0][:, s_cols].bitcast(FP8X4),
                lhsT_scale=stationary[1][:, s_cols],
                rhs=moving[0][:, m_cols].bitcast(FP8X4),
                rhs_scale=moving[1][:, m_cols],
                start=start,
                stop=stop,
            )

        down_bias = const.tile([P, ADAPTERS * ROW_TILES], F32, name="down_bias")

        def prepare_down_biases():
            bias_bank = psum.tile([P, CHUNK], F32, name="bank")
            nc.tensor.transpose(bias_bank[:, 0:P], down_bias_rows[:].bitcast(F32), identity[:])
            down_bias_words = const.tile([P, ADAPTERS * HALVES], F32, name="down_bias_words")
            nc.vector.tensor_copy(out=down_bias_words[:], in_=bias_bank[:, 0 : ADAPTERS * HALVES])
            nc.vector.tensor_copy(out=down_bias[:], in_=down_bias_words[:].bitcast(BF16))

        kv_bias = {}

        def add_biases(c):
            kv_bias[c] = const.tile([P, CHUNK], F32, name="kv_bias%d" % c)
            first = c * CHUNK - QUERY
            nc.vector.tensor_tensor(
                out=kv_bias[c][:],
                in0=up_bias[:, first : first + CHUNK],
                in1=up_bias[:, KV + first : KV + first + CHUNK],
                op=mybir.AluOpType.add,
            )

        h_rows = {}
        h_grouped = keep.tile([P, BLOCK], BF16, name="h_grouped", align_bytes=64)
        h_operand = (
            keep.tile([P, PASSES * CHUNK], U32, name="h_codes", align_bytes=64),
            keep.tile([P, PASSES * CHUNK], U8, name="h_scales", align_bytes=64),
        )

        def down_products(a):
            h_rows[a] = hidden.tile([P, ROW_TILES, TOKENS], BF16, name="h_rows")
            for t in range(ROW_TILES):
                acc = psum.tile([P, CHUNK], F32, name="bank")
                for g in range(PASSES):
                    mx_pass(acc[:], operand["down", a], t, operand["x", 0], g, g == 0, g == PASSES - 1)
                nc.scalar.activation(
                    out=h_rows[a][:, t, :],
                    in_=acc[:],
                    func=mybir.ActivationFunctionType.Tanh,
                    bias=down_bias[:, a * ROW_TILES + t : a * ROW_TILES + t + 1],
                    scale=1.0,
                )

        def group_hidden(a):
            nc.vector.tensor_copy(
                out=h_grouped[:, a * BLOCK // ADAPTERS : (a + 1) * BLOCK // ADAPTERS].rearrange(
                    "p (n t) -> p n t", t=PACK
                ),
                in_=h_rows[a][:].rearrange("p t n -> p n t"),
            )

        def in_output_order(columns, tiles=ROW_TILES):
            return columns.rearrange("p (j r) -> p r j", j=tiles)

        def as_written(columns, tiles=ROW_TILES):
            return columns.rearrange("p (r j) -> p r j", j=tiles)

        acc = {}

        def multiply(c, j, cols=range(CHUNK)):
            passes = [("x", "base", g) for g in range(PASSES)]
            if c * CHUNK >= QUERY:
                passes += [("h", "up", a) for a in range(ADAPTERS)]
            acc[c, j] = psum.tile([P, CHUNK], F32, name="bank")
            for i, (tokens, weights, g) in enumerate(passes):
                mx_pass(
                    acc[c, j][:, 0 : len(cols)], operand[tokens, 0], j, operand[weights, c], g,
                    i == 0, i == len(passes) - 1, cols,
                )

        def finish(c, j, scalar=False, cols=range(CHUNK)):
            tiles = 2 if c == last else ROW_TILES
            result = results.tile([P, CHUNK], F32, name="result")
            first = c * CHUNK + cols.start
            halves = range(cols.start, cols.stop, CHUNK // 2) if c == last else (cols.start,)
            width = CHUNK // 2 if c == last else CHUNK
            for start in halves:
                at = slice(start - cols.start, start - cols.start + width)
                target = as_written(result[:, at], tiles)
                sums = in_output_order(acc[c, j][:, at], tiles)
                if c * CHUNK >= QUERY:
                    nc.vector.tensor_tensor(
                        out=target,
                        in0=sums,
                        in1=as_written(kv_bias[c][:, start : start + width], tiles),
                        op=mybir.AluOpType.add,
                    )
                elif scalar:
                    nc.scalar.copy(out=target, in_=sums)
                else:
                    nc.vector.tensor_copy(out=target, in_=sums)
            nc.sync.dma_start(
                out=out_tiles[j, :, first : first + len(cols)], in_=result[:, 0 : len(cols)]
            )

        for name, pool, label in ((("x", 0), keep, "x"), (("down", 0), rotate, "w")):
            open_block(name, pool, label)
            for pair in range(2):
                for g in range(PASSES):
                    transpose_pair(name, g, pair, on_vector=False)
                    quantise_rows(name, g * CHUNK + 2 * pair * P, 2 * P)
        prepare_down_biases()
        down_products(0)
        transpose_block(("down", 1), vector_pairs=((0, 0), (0, 1), (1, 0)))
        for g in range(PASSES):
            quantise_rows(("down", 1), g * CHUNK, CHUNK)
        transpose_block(("base", 0))
        group_hidden(0)
        down_products(1)
        quantise(("base", 0))
        transpose_block(("base", 1))
        group_hidden(1)
        grouped["h", 0] = h_grouped
        operand["h", 0] = h_operand
        quantise(("h", 0))

        for j in range(ROW_TILES):
            multiply(0, j)
        for j in range(ROW_TILES):
            finish(0, j, scalar=j % 2 == 1)
        quantise(("base", 1))

        for c in range(QUERY // CHUNK, last + 1):
            transpose_block(("base", c), ())
            quantise(("base", c))
            transpose_block(("up", c), ())
            for j in range(ROW_TILES):
                multiply(c - 1, j)
            if c > QUERY // CHUNK:
                add_biases(c - 1)
            finish(c - 1, 0)
            finish(c - 1, 1, scalar=True)
            quantise(("up", c))
            finish(c - 1, 2)
            finish(c - 1, 3, scalar=True)
        add_biases(last)
        for j in range(ROW_TILES):
            width = CHUNK if j < ROW_TILES - 1 else CHUNK // 2
            for first in range(0, CHUNK, width):
                multiply(last, j, range(first, first + width))
                finish(last, j, cols=range(first, first + width))
